import numpy as np
import ml_dtypes


def mxq(x, axis, fmt="e4m3"):
    dtype, down = {"e4m3": (ml_dtypes.float8_e4m3fn, 7), "e5m2": (ml_dtypes.float8_e5m2, 14)}[fmt]
    v = np.moveaxis(np.asarray(x, np.float32).astype(ml_dtypes.bfloat16).astype(np.float64), axis, -1)
    blocks = v.reshape(v.shape[:-1] + (-1, 32))
    amax = np.abs(blocks).max(-1, keepdims=True)
    byte = np.maximum(np.where(amax > 0, np.frexp(amax)[1] - 1 + 127, 0) - down, 1)
    scale = np.exp2(byte - 127.0)
    codes = (blocks / scale).astype(np.float32).astype(dtype).astype(np.float64)
    return np.moveaxis((codes * scale).reshape(v.shape), -1, axis)


WIDE = False


def mx_kscale(k):
    if not WIDE:
        return np.ones(k)
    levels = np.array([10, -10, 5, -5, 0])
    if k % 512:
        return np.exp2(np.random.permutation(np.resize(levels, k // 32))).repeat(32)
    a = np.empty((k // 512, 16))
    for p in range(k // 512):
        a[p, :8] = np.random.permutation(np.resize(levels, 8))
        for g in range(8):
            far = levels[np.abs(levels - a[p, g]) >= 10]
            a[p, g + 8] = far[np.random.randint(len(far))]
    return np.exp2(a.ravel()).repeat(32)


BF16 = ml_dtypes.bfloat16


def bf(x):
    return np.asarray(x, np.float32).astype(BF16)


def f64(x):
    return np.asarray(x).astype(np.float64)


T, B, I, H = 32, 128, 512, 512


def sigmoid(v):
    return 1.0 / (1.0 + np.exp(-v))


def draw0():
    s = mx_kscale(I)
    return {
        "input": bf(np.random.standard_normal((T, B, I)) * s),
        "h0": bf(np.random.standard_normal((B, H))),
        "c0": bf(np.random.standard_normal((B, H))),
        "noise": bf(np.random.standard_normal((B, H)) * 0.3),
        "W_ih": bf(np.random.standard_normal((4 * H, I)) / np.sqrt(I) / s[None, :]),
        "W_hh": bf(np.random.standard_normal((4 * H, H)) * 0.7 / np.sqrt(H)),
        "b_ih": bf(np.random.standard_normal(4 * H) * 0.3),
        "b_hh": bf(np.random.standard_normal(4 * H) * 0.3),
    }


def core(input, h0, c0, noise, W_ih, W_hh, b_ih, b_hh):
    hsz = h0.shape[-1]
    gx = mxq(f64(input), 2, "e4m3") @ mxq(f64(W_ih), 1, "e4m3").T
    gh = f64(h0) @ f64(W_hh).T
    gates = gx + gh[None, :, :] + (f64(b_ih) + f64(b_hh))
    i_g = sigmoid(gates[..., 0 * hsz:1 * hsz])
    f_g = sigmoid(gates[..., 1 * hsz:2 * hsz])
    g_g = np.tanh(gates[..., 2 * hsz:3 * hsz])
    o_g = sigmoid(gates[..., 3 * hsz:4 * hsz])
    c = f_g * f64(c0)[None] + i_g * g_g
    h = o_g * np.tanh(c) + f64(noise)[None]
    return (h, np.stack([h[-1], c[-1]]))


def e4m3fn_bytes(y):
    return np.clip(np.asarray(y, np.float64), -448.0, 448.0).astype(np.float32).astype(ml_dtypes.float8_e4m3fn).view(np.uint8)


def e4m3fn_values(b):
    return np.asarray(b, np.uint8).view(ml_dtypes.float8_e4m3fn).astype(np.float64)


def setup_inputs():
    d = draw0()
    x0 = np.asarray(d['input']).astype(np.float64)
    s = (np.max(np.abs(x0), axis=(0, 1), keepdims=True) / 448.0).astype(np.float32)
    out = {}
    for k, v in d.items():
        if k == 'input':
            out['input_bytes'] = e4m3fn_bytes(x0 / s.astype(np.float64))
            out['input_scale'] = s
        else:
            out[k] = v
    return out


def reference(input_bytes, input_scale, h0, c0, noise, W_ih, W_hh, b_ih, b_hh):
    return core(e4m3fn_values(input_bytes) * input_scale.astype(np.float64), h0, c0, noise, W_ih, W_hh, b_ih, b_hh)

@@ -1,0 +1,272 @@
+from contextlib import ExitStack
+
+import concourse.mybir as mybir
+from concourse.masks import make_identity
+
+T, B, I, H = 32, 128, 512, 512
+FLOPS = 2 * T * B * 4 * H * I + 2 * B * 4 * H * H
+
+F32 = mybir.dt.float32
+BF16 = mybir.dt.bfloat16
+U32 = mybir.dt.uint32
+U8 = mybir.dt.uint8
+FP8 = mybir.dt.float8_e4m3fn
+FP8X4 = mybir.dt.float8_e4m3fn_x4
+ALU = mybir.AluOpType
+ACT = mybir.ActivationFunctionType
+
+P = 128
+NQ = T // 2
+V_TAIL = 1
+Z_BUFS = 5
+LEAD = 3
+XCH = (2, 6, 8, 8, 8)
+PRODS = ((0, 1), (1, 1), (2, 2), (4, 4), (8, 4), (12, 4), (16, 4), (20, 4), (24, 4), (28, 4))
+
+
+def tile_lstmlayer_kernel(tc, input_bytes, input_scale, h0, c0, noise, W_ih, W_hh, b_ih, b_hh, out_0, out_1):
+    nc = tc.nc
+    with ExitStack() as ctx:
+        const = ctx.enter_context(tc.tile_pool(name="const", bufs=1))
+        xbytes = ctx.enter_context(tc.tile_pool(name="xbytes", bufs=1))
+        stage = ctx.enter_context(tc.tile_pool(name="stage", bufs=2))
+        ps_tp = ctx.enter_context(tc.psum_pool(name="ps_tp", bufs=2))
+        ps_mm = ctx.enter_context(tc.psum_pool(name="ps_mm", bufs=4))
+        ps_cn = ctx.enter_context(tc.psum_pool(name="ps_cn", bufs=1))
+
+        sc4 = const.tile([P, 4, I], F32, name="sc4")
+        xb = []
+        xat = []
+        for c in range(len(XCH)):
+            xb.append(xbytes.tile([P, XCH[c], I], U8, name="xb%d" % c))
+            for j in range(XCH[c]):
+                xat.append((c, j))
+        c0_sb = const.tile([P, H], BF16, name="c0_sb")
+        nz_sb = const.tile([P, H], BF16, name="nz_sb")
+        ones = const.tile([P, P], BF16, name="ones")
+        warm = const.tile([P, 2], F32, name="warm")
+        ghb = const.tile([P, 4 * H], F32, name="ghb")
+        wcodes = const.tile([P, 4 * H], U32, name="wcodes", align_bytes=64)
+        wsc = const.tile([P, 4 * H], U8, name="wsc", align_bytes=64)
+        xcodes = const.tile([P, T * B], U32, name="xcodes", align_bytes=64)
+        xsc = const.tile([P, T * B], U8, name="xsc", align_bytes=64)
+        xs = const.tile([P, T, I], BF16, name="xs")
+        ident_b = const.tile([P, P], BF16, name="ident_b")
+        ident_f = const.tile([P, P], F32, name="ident_f")
+
+        def load_x(c):
+            t0 = sum(XCH[:c])
+            nc.sync.dma_start(out=xb[c][:], in_=input_bytes[t0:t0 + XCH[c]].rearrange("t b k -> b t k"))
+
+        with tc.tile_pool(name="whead", bufs=1) as whead:
+            whh = []
+            wih = []
+            for c in range(4):
+                whh.append(whead.tile([P, 4, H], BF16, name="whh%d" % c))
+                wih.append(whead.tile([P, 4, I], BF16, name="wih%d" % c))
+            h0_sb = whead.tile([P, H], BF16, name="h0_sb")
+            bt = whead.tile([P, 4 * H], BF16, name="bt")
+            h0T = whead.tile([P, 4, P], BF16, name="h0T")
+            whhT = whead.tile([P, 4, 4 * H], BF16, name="whhT")
+
+            nc.scalar.dma_start(out=sc4[:, 0, :], in_=input_scale.rearrange("a b k -> (a b k)").partition_broadcast(P))
+            nc.vector.memset(warm[:], 0.0)
+            nc.vector.memset(bt[:], 0.0)
+            nc.vector.memset(ones[:], 1.0)
+            nc.scalar.activation(out=warm[:, 1:2], in_=warm[:, 0:1], func=ACT.Sigmoid)
+
+            whh_v = W_hh.rearrange("(r p) k -> p r k", p=P)
+            wih_v = W_ih.rearrange("(r p) k -> p r k", p=P)
+            load_x(0)
+            load_x(1)
+            nc.sync.dma_start(out=h0_sb[:], in_=h0)
+            nc.sync.dma_start(out=whh[0][:], in_=whh_v[:, 0:4, :])
+            load_x(2)
+            nc.sync.dma_start(out=whh[1][:], in_=whh_v[:, 4:8, :])
+            nc.sync.dma_start(out=whh[2][:], in_=whh_v[:, 8:12, :])
+            load_x(3)
+            nc.sync.dma_start(out=whh[3][:], in_=whh_v[:, 12:16, :])
+            nc.sync.dma_start(out=wih[0][:], in_=wih_v[:, 0:4, :])
+            load_x(4)
+            for c in range(1, 4):
+                nc.sync.dma_start(out=wih[c][:], in_=wih_v[:, 4 * c:4 * c + 4, :])
+            nc.scalar.dma_start(out=bt[0:1, :], in_=b_ih.rearrange("(o n) -> o n", o=1))
+            nc.scalar.dma_start(out=bt[1:2, :], in_=b_hh.rearrange("(o n) -> o n", o=1))
+            nc.scalar.dma_start(out=c0_sb[:], in_=c0)
+            nc.scalar.dma_start(out=nz_sb[:], in_=noise)
+
+            make_identity(nc, ident_b[:])
+            make_identity(nc, ident_f[:])
+
+            nc.scalar.copy(out=sc4[:, 1, :], in_=sc4[:, 0, :])
+            nc.scalar.copy(out=sc4[:, 2:4, :], in_=sc4[:, 0:2, :])
+
+            for t0, n in PRODS:
+                c, j = xat[t0]
+                nc.vector.tensor_tensor(
+                    out=xs[:, t0:t0 + n, :].rearrange("p n k -> p (n k)"),
+                    in0=xb[c][:, j:j + n, :].rearrange("p n k -> p (n k)").bitcast(FP8),
+                    in1=sc4[:, 0:n, :].rearrange("p n k -> p (n k)"),
+                    op=ALU.mult,
+                )
+
+            pt_h = ps_tp.tile([P, 4, P], BF16, tag="tp")
+            for kt in range(4):
+                nc.tensor.transpose(pt_h[:, kt, :], h0_sb[:, kt * P:(kt + 1) * P], ident_b[:])
+            nc.scalar.copy(out=h0T[:], in_=pt_h[:])
+            for c in range(4):
+                cols = slice(c * 512, (c + 1) * 512)
+                for half in range(2):
+                    pt_w = ps_tp.tile([P, 2, 512], BF16, tag="tp")
+                    for kk in range(2):
+                        kt = 2 * half + kk
+                        for r in range(4):
+                            nc.tensor.transpose(pt_w[:, kk, r * P:(r + 1) * P], whh[c][:, r, kt * P:(kt + 1) * P], ident_b[:])
+                    nc.scalar.copy(out=whhT[:, 2 * half:2 * half + 2, cols], in_=pt_w[:])
+                gp = ps_mm.tile([P, 512], F32, tag="mm")
+                for kt in range(4):
+                    nc.tensor.matmul(gp[:], lhsT=h0T[:, kt, :], rhs=whhT[:, kt, cols], start=(kt == 0), stop=False)
+                nc.tensor.matmul(gp[:], lhsT=ones[:], rhs=bt[:, cols], start=False, stop=True)
+                nc.scalar.copy(out=ghb[:, cols], in_=gp[:])
+
+            for c in range(4):
+                cols = slice(c * 512, (c + 1) * 512)
+                wg = stage.tile([P, 2048], BF16, tag="wg", align_bytes=64)
+                wwords = wih[c][:].bitcast(F32)
+                wgw = wg[:].bitcast(F32)
+                for rp in range(2):
+                    pt_i = ps_tp.tile([P, 2, 2, P], F32, tag="tp")
+                    for r2 in range(2):
+                        for u in range(2):
+                            nc.tensor.transpose(pt_i[:, r2, u, :], wwords[:, 2 * rp + r2, u:256:2], ident_f[:])
+                    nc.scalar.copy(
+                        out=wgw[:, rp * 512:(rp + 1) * 512].rearrange("p (r n u) -> p r n u", r=2, u=2),
+                        in_=pt_i[:].rearrange("p r u n -> p r n u"),
+                    )
+                nc.vector.quantize_mx(out=wcodes[:, cols].bitcast(FP8X4), scales=wsc[:, cols], in_=wg[:])
+
+        zpool = ctx.enter_context(tc.tile_pool(name="zpool", bufs=Z_BUFS))
+
+        c0_ps = ps_cn.tile([P, H], F32, name="c0_ps")
+        nc.tensor.matmul(c0_ps[:], lhsT=ident_b[:], rhs=c0_sb[:], start=True, stop=True)
+        nz_ps = ps_cn.tile([P, H], F32, name="nz_ps")
+        nc.tensor.matmul(nz_ps[:], lhsT=ident_b[:], rhs=nz_sb[:], start=True, stop=True)
+
+        pts = {}
+        xgs = {}
+        done_q = set()
+
+        def turn_t(q):
+            if not 0 <= q < NQ:
+                return
+            xwords = xs[:, 2 * q:2 * q + 2, :].bitcast(F32)
+            pt_x = ps_tp.tile([P, 2, 2, P], F32, tag="tp")
+            pts[q] = pt_x
+            for j in range(2):
+                for u in range(2):
+                    nc.tensor.transpose(pt_x[:, j, u, :], xwords[:, j, u:256:2], ident_f[:])
+
+        def turn_e(q):
+            if not 0 <= q < NQ:
+                return
+            xg = stage.tile([P, 1024], BF16, tag="xg", align_bytes=64)
+            xgs[q] = xg
+            nc.scalar.copy(
+                out=xg[:].bitcast(F32).rearrange("p (r n u) -> p r n u", r=2, u=2),
+                in_=pts[q][:].rearrange("p r u n -> p r n u"),
+            )
+
+        def turn_q(q):
+            if not 0 <= q < NQ or q in done_q:
+                return
+            done_q.add(q)
+            qc = slice(q * 256, (q + 1) * 256)
+            nc.vector.quantize_mx(out=xcodes[:, qc].bitcast(FP8X4), scales=xsc[:, qc], in_=xgs[q][:])
+
+        zs = {}
+        SI, SF, SO, SG = (slice(0, 512), slice(512, 1024), slice(1024, 1536), slice(1536, 2048))
+        GATE = {"f": (SF, 1, ACT.Sigmoid), "i": (SI, 0, ACT.Sigmoid), "g": (SG, 2, ACT.Tanh), "o": (SO, 3, ACT.Sigmoid)}
+
+        def eng(m):
+            if m < NQ - V_TAIL:
+                return nc.gpsimd
+            return nc.vector
+
+        def ok(m):
+            return 0 <= m < NQ
+
+        def gate(x, t):
+            m = t // 2
+            if m not in zs:
+                z_new = zpool.tile([P, 2, 2048], F32, tag="z")
+                zs[m] = z_new
+            z = zs[m]
+            dst, gb, fn = GATE[x]
+            tcols = slice(t * P, (t + 1) * P)
+            cols = slice(gb * 512, (gb + 1) * 512)
+            acc = ps_mm.tile([P, 512], F32, tag="mm")
+            nc.tensor.matmul_mx(
+                out=acc[:],
+                lhsT=xcodes[:, tcols].bitcast(FP8X4), lhsT_scale=xsc[:, tcols],
+                rhs=wcodes[:, cols].bitcast(FP8X4), rhs_scale=wsc[:, cols],
+                start=True, stop=True,
+            )
+            nc.vector.tensor_tensor(out=z[:, t % 2, dst], in0=acc[:], in1=ghb[:, cols], op=ALU.add)
+            nc.scalar.activation(out=z[:, t % 2, dst], in_=z[:, t % 2, dst], func=fn)
+
+        def both(ps_tile):
+            return ps_tile[:].unsqueeze(1).to_broadcast([P, 2, H])
+
+        def op_v(m):
+            if ok(m):
+                nc.vector.tensor_tensor(out=zs[m][:, :, SF], in0=zs[m][:, :, SF], in1=both(c0_ps), op=ALU.mult)
+
+        def op_u(m):
+            if ok(m):
+                eng(m).tensor_tensor(out=zs[m][:, :, SI], in0=zs[m][:, :, SI], in1=zs[m][:, :, SG], op=ALU.mult)
+
+        def op_c(m):
+            if ok(m):
+                eng(m).tensor_tensor(out=zs[m][:, :, SI], in0=zs[m][:, :, SI], in1=zs[m][:, :, SF], op=ALU.add)
+
+        def op_tc(m):
+            if ok(m):
+                nc.scalar.activation(out=zs[m][:, :, SG], in_=zs[m][:, :, SI], func=ACT.Tanh)
+
+        def op_w(m):
+            if ok(m):
+                eng(m).tensor_tensor(out=zs[m][:, :, SO], in0=zs[m][:, :, SO], in1=zs[m][:, :, SG], op=ALU.mult)
+
+        def op_h(m):
+            if not ok(m):
+                return
+            z = zs[m]
+            nc.vector.tensor_tensor(out=z[:, :, SO], in0=z[:, :, SO], in1=both(nz_ps), op=ALU.add)
+            nc.sync.dma_start(out=out_0[2 * m:2 * m + 2].rearrange("t b j -> b t j"), in_=z[:, :, SO])
+            if m == NQ - 1:
+                nc.sync.dma_start(out=out_1[0], in_=z[:, 1, SO])
+                nc.sync.dma_start(out=out_1[1], in_=z[:, 1, SI])
+
+        for q in range(LEAD):
+            turn_t(q)
+            turn_e(q)
+            turn_q(q)
+        with tc.manual_schedule():
+            for m in range(NQ + 4):
+                op_v(m - 1)
+                if ok(m):
+                    gate("f", 2 * m)
+                    gate("i", 2 * m)
+                op_tc(m - 2)
+                if ok(m):
+                    gate("g", 2 * m)
+                    gate("o", 2 * m)
+                    turn_t(m + LEAD)
+                    for x in ("f", "i", "g", "o"):
+                        gate(x, 2 * m + 1)
+                    turn_e(m + LEAD)
+                    turn_q(m + LEAD - 1)
+                op_w(m - 3)
+                op_u(m - 1)
+                op_c(m - 1)
+                op_h(m - 3)

@@ -18,10 +18,11 @@ ACT = mybir.ActivationFunctionType
 P = 128
 NQ = T // 2
 V_TAIL = 1
-Z_BUFS = 5
 LEAD = 3
 XCH = (2, 6, 8, 8, 8)
 PRODS = ((0, 1), (1, 1), (2, 2), (4, 4), (8, 4), (12, 4), (16, 4), (20, 4), (24, 4), (28, 4))
+ROWS = {"i": 0, "f": 1, "g": 2, "o": 3}
+SLOT = {"f": 0, "i": 1, "g": 2}
 
 
 def tile_lstmlayer_kernel(tc, input_bytes, input_scale, h0, c0, noise, W_ih, W_hh, b_ih, b_hh, out_0, out_1):
@@ -30,8 +31,8 @@ def tile_lstmlayer_kernel(tc, input_bytes, input_scale, h0, c0, noise, W_ih, W_h
         const = ctx.enter_context(tc.tile_pool(name="const", bufs=1))
         xbytes = ctx.enter_context(tc.tile_pool(name="xbytes", bufs=1))
         stage = ctx.enter_context(tc.tile_pool(name="stage", bufs=2))
-        ps_tp = ctx.enter_context(tc.psum_pool(name="ps_tp", bufs=2))
-        ps_mm = ctx.enter_context(tc.psum_pool(name="ps_mm", bufs=4))
+        ps_tp = ctx.enter_context(tc.psum_pool(name="ps_tp", bufs=1))
+        ps_mm = ctx.enter_context(tc.psum_pool(name="ps_mm", bufs=3))
         ps_cn = ctx.enter_context(tc.psum_pool(name="ps_cn", bufs=1))
 
         sc4 = const.tile([P, 4, I], F32, name="sc4")
@@ -45,7 +46,8 @@ def tile_lstmlayer_kernel(tc, input_bytes, input_scale, h0, c0, noise, W_ih, W_h
         nz_sb = const.tile([P, H], BF16, name="nz_sb")
         ones = const.tile([P, P], BF16, name="ones")
         warm = const.tile([P, 2], F32, name="warm")
-        ghb = const.tile([P, 4 * H], F32, name="ghb")
+        ghbT = const.tile([P, 3, 4, P], F32, name="ghbT")
+        ghbo = const.tile([P, H], F32, name="ghbo")
         wcodes = const.tile([P, 4 * H], U32, name="wcodes", align_bytes=64)
         wsc = const.tile([P, 4 * H], U8, name="wsc", align_bytes=64)
         xcodes = const.tile([P, T * B], U32, name="xcodes", align_bytes=64)
@@ -58,12 +60,12 @@ def tile_lstmlayer_kernel(tc, input_bytes, input_scale, h0, c0, noise, W_ih, W_h
             t0 = sum(XCH[:c])
             nc.sync.dma_start(out=xb[c][:], in_=input_bytes[t0:t0 + XCH[c]].rearrange("t b k -> b t k"))
 
-        with tc.tile_pool(name="whead", bufs=1) as whead:
-            whh = []
-            wih = []
-            for c in range(4):
-                whh.append(whead.tile([P, 4, H], BF16, name="whh%d" % c))
-                wih.append(whead.tile([P, 4, I], BF16, name="wih%d" % c))
+        with tc.tile_pool(name="whead", bufs=1) as whead, tc.psum_pool(name="ps_hd", bufs=2) as ps_hd:
+            whh = {}
+            wih = {}
+            for x in "figo":
+                whh[x] = whead.tile([P, 4, H], BF16, name="whh_" + x)
+                wih[x] = whead.tile([P, 4, I], BF16, name="wih_" + x)
             h0_sb = whead.tile([P, H], BF16, name="h0_sb")
             bt = whead.tile([P, 4 * H], BF16, name="bt")
             h0T = whead.tile([P, 4, P], BF16, name="h0T")
@@ -77,19 +79,24 @@ def tile_lstmlayer_kernel(tc, input_bytes, input_scale, h0, c0, noise, W_ih, W_h
 
             whh_v = W_hh.rearrange("(r p) k -> p r k", p=P)
             wih_v = W_ih.rearrange("(r p) k -> p r k", p=P)
+
+            def load_w(dst, view, x):
+                nc.sync.dma_start(out=dst[x][:], in_=view[:, 4 * ROWS[x]:4 * ROWS[x] + 4, :])
+
             load_x(0)
             load_x(1)
             nc.sync.dma_start(out=h0_sb[:], in_=h0)
-            nc.sync.dma_start(out=whh[0][:], in_=whh_v[:, 0:4, :])
+            load_w(whh, whh_v, "f")
+            load_w(wih, wih_v, "f")
             load_x(2)
-            nc.sync.dma_start(out=whh[1][:], in_=whh_v[:, 4:8, :])
-            nc.sync.dma_start(out=whh[2][:], in_=whh_v[:, 8:12, :])
+            load_w(whh, whh_v, "i")
+            load_w(wih, wih_v, "i")
             load_x(3)
-            nc.sync.dma_start(out=whh[3][:], in_=whh_v[:, 12:16, :])
-            nc.sync.dma_start(out=wih[0][:], in_=wih_v[:, 0:4, :])
+            load_w(whh, whh_v, "g")
+            load_w(wih, wih_v, "g")
             load_x(4)
-            for c in range(1, 4):
-                nc.sync.dma_start(out=wih[c][:], in_=wih_v[:, 4 * c:4 * c + 4, :])
+            load_w(whh, whh_v, "o")
+            load_w(wih, wih_v, "o")
             nc.scalar.dma_start(out=bt[0:1, :], in_=b_ih.rearrange("(o n) -> o n", o=1))
             nc.scalar.dma_start(out=bt[1:2, :], in_=b_hh.rearrange("(o n) -> o n", o=1))
             nc.scalar.dma_start(out=c0_sb[:], in_=c0)
@@ -110,32 +117,39 @@ def tile_lstmlayer_kernel(tc, input_bytes, input_scale, h0, c0, noise, W_ih, W_h
                     op=ALU.mult,
                 )
 
-            pt_h = ps_tp.tile([P, 4, P], BF16, tag="tp")
+            pt_h = ps_hd.tile([P, 4, P], BF16, tag="hd")
             for kt in range(4):
                 nc.tensor.transpose(pt_h[:, kt, :], h0_sb[:, kt * P:(kt + 1) * P], ident_b[:])
             nc.scalar.copy(out=h0T[:], in_=pt_h[:])
-            for c in range(4):
-                cols = slice(c * 512, (c + 1) * 512)
+
+            for x in "figo":
+                cols = slice(ROWS[x] * 512, (ROWS[x] + 1) * 512)
                 for half in range(2):
-                    pt_w = ps_tp.tile([P, 2, 512], BF16, tag="tp")
+                    pt_w = ps_hd.tile([P, 2, 512], BF16, tag="hd")
                     for kk in range(2):
                         kt = 2 * half + kk
                         for r in range(4):
-                            nc.tensor.transpose(pt_w[:, kk, r * P:(r + 1) * P], whh[c][:, r, kt * P:(kt + 1) * P], ident_b[:])
+                            nc.tensor.transpose(pt_w[:, kk, r * P:(r + 1) * P], whh[x][:, r, kt * P:(kt + 1) * P], ident_b[:])
                     nc.scalar.copy(out=whhT[:, 2 * half:2 * half + 2, cols], in_=pt_w[:])
-                gp = ps_mm.tile([P, 512], F32, tag="mm")
-                for kt in range(4):
-                    nc.tensor.matmul(gp[:], lhsT=h0T[:, kt, :], rhs=whhT[:, kt, cols], start=(kt == 0), stop=False)
-                nc.tensor.matmul(gp[:], lhsT=ones[:], rhs=bt[:, cols], start=False, stop=True)
-                nc.scalar.copy(out=ghb[:, cols], in_=gp[:])
-
-            for c in range(4):
-                cols = slice(c * 512, (c + 1) * 512)
+                if x == "o":
+                    gp = ps_mm.tile([P, 512], F32, tag="mm")
+                    for kt in range(4):
+                        nc.tensor.matmul(gp[:], lhsT=h0T[:, kt, :], rhs=whhT[:, kt, cols], start=(kt == 0), stop=False)
+                    nc.tensor.matmul(gp[:], lhsT=ones[:], rhs=bt[:, cols], start=False, stop=True)
+                    nc.scalar.copy(out=ghbo[:], in_=gp[:])
+                else:
+                    gq = ps_mm.tile([P, 4, P], F32, tag="mm")
+                    for jt in range(4):
+                        jc = slice(cols.start + jt * P, cols.start + (jt + 1) * P)
+                        for kt in range(4):
+                            nc.tensor.matmul(gq[:, jt, :], lhsT=whhT[:, kt, jc], rhs=h0T[:, kt, :], start=(kt == 0), stop=False)
+                        nc.tensor.matmul(gq[:, jt, :], lhsT=bt[:, jc], rhs=ones[:], start=False, stop=True)
+                    nc.scalar.copy(out=ghbT[:, SLOT[x], :, :], in_=gq[:])
                 wg = stage.tile([P, 2048], BF16, tag="wg", align_bytes=64)
-                wwords = wih[c][:].bitcast(F32)
+                wwords = wih[x][:].bitcast(F32)
                 wgw = wg[:].bitcast(F32)
                 for rp in range(2):
-                    pt_i = ps_tp.tile([P, 2, 2, P], F32, tag="tp")
+                    pt_i = ps_hd.tile([P, 2, 2, P], F32, tag="hd")
                     for r2 in range(2):
                         for u in range(2):
                             nc.tensor.transpose(pt_i[:, r2, u, :], wwords[:, 2 * rp + r2, u:256:2], ident_f[:])
@@ -145,19 +159,25 @@ def tile_lstmlayer_kernel(tc, input_bytes, input_scale, h0, c0, noise, W_ih, W_h
                     )
                 nc.vector.quantize_mx(out=wcodes[:, cols].bitcast(FP8X4), scales=wsc[:, cols], in_=wg[:])
 
-        zpool = ctx.enter_context(tc.tile_pool(name="zpool", bufs=Z_BUFS))
+        ps_c = ctx.enter_context(tc.psum_pool(name="ps_c", bufs=2))
+        ztp = ctx.enter_context(tc.tile_pool(name="ztp", bufs=3))
+        zop = ctx.enter_context(tc.tile_pool(name="zop", bufs=6))
+        tcp = ctx.enter_context(tc.tile_pool(name="tcp", bufs=2))
 
-        c0_ps = ps_cn.tile([P, H], F32, name="c0_ps")
-        nc.tensor.matmul(c0_ps[:], lhsT=ident_b[:], rhs=c0_sb[:], start=True, stop=True)
+        c0T_ps = ps_cn.tile([P, 4, P], F32, name="c0T_ps")
+        for jt in range(4):
+            nc.tensor.matmul(c0T_ps[:, jt, :], lhsT=c0_sb[:, jt * P:(jt + 1) * P], rhs=ident_b[:], start=True, stop=True)
         nz_ps = ps_cn.tile([P, H], F32, name="nz_ps")
         nc.tensor.matmul(nz_ps[:], lhsT=ident_b[:], rhs=nz_sb[:], start=True, stop=True)
 
         pts = {}
         xgs = {}
-        done_q = set()
+
+        def ok(m):
+            return 0 <= m < NQ
 
         def turn_t(q):
-            if not 0 <= q < NQ:
+            if not ok(q):
                 return
             xwords = xs[:, 2 * q:2 * q + 2, :].bitcast(F32)
             pt_x = ps_tp.tile([P, 2, 2, P], F32, tag="tp")
@@ -167,7 +187,7 @@ def tile_lstmlayer_kernel(tc, input_bytes, input_scale, h0, c0, noise, W_ih, W_h
                     nc.tensor.transpose(pt_x[:, j, u, :], xwords[:, j, u:256:2], ident_f[:])
 
         def turn_e(q):
-            if not 0 <= q < NQ:
+            if not ok(q):
                 return
             xg = stage.tile([P, 1024], BF16, tag="xg", align_bytes=64)
             xgs[q] = xg
@@ -177,33 +197,57 @@ def tile_lstmlayer_kernel(tc, input_bytes, input_scale, h0, c0, noise, W_ih, W_h
             )
 
         def turn_q(q):
-            if not 0 <= q < NQ or q in done_q:
+            if not ok(q):
                 return
-            done_q.add(q)
             qc = slice(q * 256, (q + 1) * 256)
             nc.vector.quantize_mx(out=xcodes[:, qc].bitcast(FP8X4), scales=xsc[:, qc], in_=xgs[q][:])
 
-        zs = {}
-        SI, SF, SO, SG = (slice(0, 512), slice(512, 1024), slice(1024, 1536), slice(1536, 2048))
-        GATE = {"f": (SF, 1, ACT.Sigmoid), "i": (SI, 0, ACT.Sigmoid), "g": (SG, 2, ACT.Tanh), "o": (SO, 3, ACT.Sigmoid)}
+        zts = {}
+        zos = {}
+        tcs = {}
+        cps = {}
 
         def eng(m):
             if m < NQ - V_TAIL:
                 return nc.gpsimd
             return nc.vector
 
-        def ok(m):
-            return 0 <= m < NQ
+        def gate_t(x, m):
+            if not ok(m):
+                return
+            if m not in zts:
+                zt_new = ztp.tile([P, 3, 4, 2, P], F32, tag="zt")
+                zts[m] = zt_new
+            zt = zts[m]
+            gs = SLOT[x]
+            qc = slice(m * 256, (m + 1) * 256)
+            for half in range(2):
+                acc = ps_mm.tile([P, 2, 2, P], F32, tag="mm")
+                for e in range(2):
+                    jc = slice(ROWS[x] * 512 + (2 * half + e) * P, ROWS[x] * 512 + (2 * half + e + 1) * P)
+                    nc.tensor.matmul_mx(
+                        out=acc[:, e, :, :].rearrange("p t b -> p (t b)"),
+                        lhsT=wcodes[:, jc].bitcast(FP8X4), lhsT_scale=wsc[:, jc],
+                        rhs=xcodes[:, qc].bitcast(FP8X4), rhs_scale=xsc[:, qc],
+                        start=True, stop=True,
+                    )
+                nc.vector.tensor_tensor(
+                    out=zt[:, gs, 2 * half:2 * half + 2, :, :], in0=acc[:],
+                    in1=ghbT[:, gs, 2 * half:2 * half + 2, :].unsqueeze(2).to_broadcast([P, 2, 2, P]), op=ALU.add,
+                )
+            fn = ACT.Tanh if x == "g" else ACT.Sigmoid
+            nc.scalar.activation(out=zt[:, gs, :, :, :], in_=zt[:, gs, :, :, :], func=fn)
 
-        def gate(x, t):
+        def gate_o(t):
             m = t // 2
-            if m not in zs:
-                z_new = zpool.tile([P, 2, 2048], F32, tag="z")
-                zs[m] = z_new
-            z = zs[m]
-            dst, gb, fn = GATE[x]
+            if not ok(m):
+                return
+            if m not in zos:
+                zo_new = zop.tile([P, 2, H], F32, tag="zo")
+                zos[m] = zo_new
+            zo = zos[m]
             tcols = slice(t * P, (t + 1) * P)
-            cols = slice(gb * 512, (gb + 1) * 512)
+            cols = slice(ROWS["o"] * 512, (ROWS["o"] + 1) * 512)
             acc = ps_mm.tile([P, 512], F32, tag="mm")
             nc.tensor.matmul_mx(
                 out=acc[:],
@@ -211,62 +255,71 @@ def tile_lstmlayer_kernel(tc, input_bytes, input_scale, h0, c0, noise, W_ih, W_h
                 rhs=wcodes[:, cols].bitcast(FP8X4), rhs_scale=wsc[:, cols],
                 start=True, stop=True,
             )
-            nc.vector.tensor_tensor(out=z[:, t % 2, dst], in0=acc[:], in1=ghb[:, cols], op=ALU.add)
-            nc.scalar.activation(out=z[:, t % 2, dst], in_=z[:, t % 2, dst], func=fn)
-
-        def both(ps_tile):
-            return ps_tile[:].unsqueeze(1).to_broadcast([P, 2, H])
+            nc.vector.tensor_tensor(out=zo[:, t % 2, :], in0=acc[:], in1=ghbo[:], op=ALU.add)
+            nc.scalar.activation(out=zo[:, t % 2, :], in_=zo[:, t % 2, :], func=ACT.Sigmoid)
 
         def op_v(m):
             if ok(m):
-                nc.vector.tensor_tensor(out=zs[m][:, :, SF], in0=zs[m][:, :, SF], in1=both(c0_ps), op=ALU.mult)
+                f_t = zts[m][:, SLOT["f"], :, :, :]
+                nc.vector.tensor_tensor(out=f_t, in0=f_t, in1=c0T_ps[:].unsqueeze(2).to_broadcast([P, 4, 2, P]), op=ALU.mult)
 
         def op_u(m):
             if ok(m):
-                eng(m).tensor_tensor(out=zs[m][:, :, SI], in0=zs[m][:, :, SI], in1=zs[m][:, :, SG], op=ALU.mult)
+                i_t = zts[m][:, SLOT["i"], :, :, :]
+                eng(m).tensor_tensor(out=i_t, in0=i_t, in1=zts[m][:, SLOT["g"], :, :, :], op=ALU.mult)
 
         def op_c(m):
-            if ok(m):
-                eng(m).tensor_tensor(out=zs[m][:, :, SI], in0=zs[m][:, :, SI], in1=zs[m][:, :, SF], op=ALU.add)
+            if not ok(m):
+                return
+            for j in range(2):
+                cp = ps_c.tile([P, H], F32, tag="c")
+                cps[2 * m + j] = cp
+                for jt in range(4):
+                    for x in "fi":
+                        nc.tensor.matmul(cp[:, jt * P:(jt + 1) * P], lhsT=zts[m][:, SLOT[x], jt, j, :], rhs=ident_f[:], is_transpose=True, start=(x == "f"), stop=(x == "i"))
 
-        def op_tc(m):
-            if ok(m):
-                nc.scalar.activation(out=zs[m][:, :, SG], in_=zs[m][:, :, SI], func=ACT.Tanh)
+        def op_th(m):
+            if not ok(m):
+                return
+            tc_new = tcp.tile([P, 2, H], F32, tag="tc")
+            tcs[m] = tc_new
+            for j in range(2):
+                nc.scalar.activation(out=tc_new[:, j, :], in_=cps[2 * m + j][:], func=ACT.Tanh)
+            if m == NQ - 1:
+                c_last = const.tile([P, H], F32, name="c_last")
+                nc.scalar.copy(out=c_last[:], in_=cps[2 * m + 1][:])
+                nc.sync.dma_start(out=out_1[1], in_=c_last[:])
 
         def op_w(m):
             if ok(m):
-                eng(m).tensor_tensor(out=zs[m][:, :, SO], in0=zs[m][:, :, SO], in1=zs[m][:, :, SG], op=ALU.mult)
+                eng(m).tensor_tensor(out=zos[m][:], in0=zos[m][:], in1=tcs[m][:], op=ALU.mult)
 
         def op_h(m):
             if not ok(m):
                 return
-            z = zs[m]
-            nc.vector.tensor_tensor(out=z[:, :, SO], in0=z[:, :, SO], in1=both(nz_ps), op=ALU.add)
-            nc.sync.dma_start(out=out_0[2 * m:2 * m + 2].rearrange("t b j -> b t j"), in_=z[:, :, SO])
+            zo = zos[m]
+            nc.vector.tensor_tensor(out=zo[:], in0=zo[:], in1=nz_ps[:].unsqueeze(1).to_broadcast([P, 2, H]), op=ALU.add)
+            nc.sync.dma_start(out=out_0[2 * m:2 * m + 2].rearrange("t b j -> b t j"), in_=zo[:])
             if m == NQ - 1:
-                nc.sync.dma_start(out=out_1[0], in_=z[:, 1, SO])
-                nc.sync.dma_start(out=out_1[1], in_=z[:, 1, SI])
+                nc.sync.dma_start(out=out_1[0], in_=zo[:, 1, :])
 
         for q in range(LEAD):
             turn_t(q)
             turn_e(q)
             turn_q(q)
         with tc.manual_schedule():
-            for m in range(NQ + 4):
+            for m in range(NQ + 5):
+                op_h(m - 4)
+                turn_q(m + LEAD - 1)
                 op_v(m - 1)
-                if ok(m):
-                    gate("f", 2 * m)
-                    gate("i", 2 * m)
-                op_tc(m - 2)
-                if ok(m):
-                    gate("g", 2 * m)
-                    gate("o", 2 * m)
-                    turn_t(m + LEAD)
-                    for x in ("f", "i", "g", "o"):
-                        gate(x, 2 * m + 1)
-                    turn_e(m + LEAD)
-                    turn_q(m + LEAD - 1)
-                op_w(m - 3)
                 op_u(m - 1)
-                op_c(m - 1)
-                op_h(m - 3)
+                gate_t("f", m)
+                op_c(m - 2)
+                turn_t(m + LEAD)
+                turn_e(m + LEAD)
+                op_th(m - 2)
+                op_w(m - 2)
+                gate_t("i", m)
+                gate_t("g", m)
+                gate_o(2 * m)
+                gate_o(2 * m + 1)

@@ -167,6 +167,9 @@ def tile_lstmlayer_kernel(tc, input_bytes, input_scale, h0, c0, noise, W_ih, W_h
         c0T_ps = ps_cn.tile([P, 4, P], F32, name="c0T_ps")
         for jt in range(4):
             nc.tensor.matmul(c0T_ps[:, jt, :], lhsT=c0_sb[:, jt * P:(jt + 1) * P], rhs=ident_b[:], start=True, stop=True)
+        c0T2 = const.tile([P, 4, 2, P], F32, name="c0T2")
+        for j in range(2):
+            nc.scalar.copy(out=c0T2[:, :, j, :], in_=c0T_ps[:])
         nz_ps = ps_cn.tile([P, H], F32, name="nz_ps")
         nc.tensor.matmul(nz_ps[:], lhsT=ident_b[:], rhs=nz_sb[:], start=True, stop=True)
 
@@ -261,7 +264,7 @@ def tile_lstmlayer_kernel(tc, input_bytes, input_scale, h0, c0, noise, W_ih, W_h
         def op_v(m):
             if ok(m):
                 f_t = zts[m][:, SLOT["f"], :, :, :]
-                nc.vector.tensor_tensor(out=f_t, in0=f_t, in1=c0T_ps[:].unsqueeze(2).to_broadcast([P, 4, 2, P]), op=ALU.mult)
+                eng(m).tensor_tensor(out=f_t, in0=f_t, in1=c0T2[:], op=ALU.mult)
 
         def op_u(m):
             if ok(m):

@@ -18,6 +18,7 @@ ACT = mybir.ActivationFunctionType
 P = 128
 NQ = T // 2
 V_TAIL = 1
+V_EVERY = 4
 LEAD = 3
 XCH = (2, 6, 8, 8, 8)
 PRODS = ((0, 1), (1, 1), (2, 2), (4, 4), (8, 4), (12, 4), (16, 4), (20, 4), (24, 4), (28, 4))
@@ -264,7 +265,10 @@ def tile_lstmlayer_kernel(tc, input_bytes, input_scale, h0, c0, noise, W_ih, W_h
         def op_v(m):
             if ok(m):
                 f_t = zts[m][:, SLOT["f"], :, :, :]
-                eng(m).tensor_tensor(out=f_t, in0=f_t, in1=c0T2[:], op=ALU.mult)
+                if m % V_EVERY == V_EVERY - 1 or m >= NQ - V_TAIL:
+                    nc.vector.tensor_tensor(out=f_t, in0=f_t, in1=c0T_ps[:].unsqueeze(2).to_broadcast([P, 4, 2, P]), op=ALU.mult)
+                else:
+                    nc.gpsimd.tensor_tensor(out=f_t, in0=f_t, in1=c0T2[:], op=ALU.mult)
 
         def op_u(m):
             if ok(m):

@@ -239,8 +239,11 @@ def tile_lstmlayer_kernel(tc, input_bytes, input_scale, h0, c0, noise, W_ih, W_h
                     out=zt[:, gs, 2 * half:2 * half + 2, :, :], in0=acc[:],
                     in1=ghbT[:, gs, 2 * half:2 * half + 2, :].unsqueeze(2).to_broadcast([P, 2, 2, P]), op=ALU.add,
                 )
-            fn = ACT.Tanh if x == "g" else ACT.Sigmoid
-            nc.scalar.activation(out=zt[:, gs, :, :, :], in_=zt[:, gs, :, :, :], func=fn)
+            if x == "g":
+                nc.scalar.activation(out=zt[:, gs, :, :, :], in_=zt[:, gs, :, :, :], func=ACT.Tanh)
+            if x == "i":
+                fi = zt[:, 0:2, :, :, :].rearrange("p s j t b -> p (s j t b)")
+                nc.scalar.activation(out=fi, in_=fi, func=ACT.Sigmoid)
 
         def gate_o(t):
             m = t // 2
@@ -260,7 +263,8 @@ def tile_lstmlayer_kernel(tc, input_bytes, input_scale, h0, c0, noise, W_ih, W_h
                 start=True, stop=True,
             )
             nc.vector.tensor_tensor(out=zo[:, t % 2, :], in0=acc[:], in1=ghbo[:], op=ALU.add)
-            nc.scalar.activation(out=zo[:, t % 2, :], in_=zo[:, t % 2, :], func=ACT.Sigmoid)
+            if t % 2 == 1:
+                nc.scalar.activation(out=zo[:], in_=zo[:], func=ACT.Sigmoid)
 
         def op_v(m):
             if ok(m):

@@ -18,7 +18,7 @@ ACT = mybir.ActivationFunctionType
 P = 128
 NQ = T // 2
 V_TAIL = 1
-V_EVERY = 4
+V_BLOCKS = 1
 LEAD = 3
 XCH = (2, 6, 8, 8, 8)
 PRODS = ((0, 1), (1, 1), (2, 2), (4, 4), (8, 4), (12, 4), (16, 4), (20, 4), (24, 4), (28, 4))
@@ -269,10 +269,10 @@ def tile_lstmlayer_kernel(tc, input_bytes, input_scale, h0, c0, noise, W_ih, W_h
         def op_v(m):
             if ok(m):
                 f_t = zts[m][:, SLOT["f"], :, :, :]
-                if m % V_EVERY == V_EVERY - 1 or m >= NQ - V_TAIL:
-                    nc.vector.tensor_tensor(out=f_t, in0=f_t, in1=c0T_ps[:].unsqueeze(2).to_broadcast([P, 4, 2, P]), op=ALU.mult)
-                else:
-                    nc.gpsimd.tensor_tensor(out=f_t, in0=f_t, in1=c0T2[:], op=ALU.mult)
+                vj = 4 if m >= NQ - V_TAIL else V_BLOCKS
+                nc.vector.tensor_tensor(out=f_t[:, 0:vj], in0=f_t[:, 0:vj], in1=c0T_ps[:, 0:vj, :].unsqueeze(2).to_broadcast([P, vj, 2, P]), op=ALU.mult)
+                if vj < 4:
+                    nc.gpsimd.tensor_tensor(out=f_t[:, vj:4], in0=f_t[:, vj:4], in1=c0T2[:, vj:4], op=ALU.mult)
 
         def op_u(m):
             if ok(m):

@@ -57,6 +57,12 @@ def tile_lstmlayer_kernel(tc, input_bytes, input_scale, h0, c0, noise, W_ih, W_h
         ident_b = const.tile([P, P], BF16, name="ident_b")
         ident_f = const.tile([P, P], F32, name="ident_f")
 
+        wgs = {}
+
+        def quant_w(x):
+            cols = slice(ROWS[x] * 512, (ROWS[x] + 1) * 512)
+            nc.vector.quantize_mx(out=wcodes[:, cols].bitcast(FP8X4), scales=wsc[:, cols], in_=wgs[x][:])
+
         def load_x(c):
             t0 = sum(XCH[:c])
             nc.sync.dma_start(out=xb[c][:], in_=input_bytes[t0:t0 + XCH[c]].rearrange("t b k -> b t k"))
@@ -158,7 +164,9 @@ def tile_lstmlayer_kernel(tc, input_bytes, input_scale, h0, c0, noise, W_ih, W_h
                         out=wgw[:, rp * 512:(rp + 1) * 512].rearrange("p (r n u) -> p r n u", r=2, u=2),
                         in_=pt_i[:].rearrange("p r u n -> p r n u"),
                     )
-                nc.vector.quantize_mx(out=wcodes[:, cols].bitcast(FP8X4), scales=wsc[:, cols], in_=wg[:])
+                wgs[x] = wg
+                if x != "o":
+                    quant_w(x)
 
         ps_c = ctx.enter_context(tc.psum_pool(name="ps_c", bufs=2))
         ztp = ctx.enter_context(tc.tile_pool(name="ztp", bufs=3))
@@ -317,7 +325,8 @@ def tile_lstmlayer_kernel(tc, input_bytes, input_scale, h0, c0, noise, W_ih, W_h
         for q in range(LEAD):
             turn_t(q)
             turn_e(q)
-            turn_q(q)
+            if q < LEAD - 1:
+                turn_q(q)
         with tc.manual_schedule():
             for m in range(NQ + 5):
                 op_h(m - 4)
@@ -331,6 +340,8 @@ def tile_lstmlayer_kernel(tc, input_bytes, input_scale, h0, c0, noise, W_ih, W_h
                 op_th(m - 2)
                 op_w(m - 2)
                 gate_t("i", m)
+                if m == 0:
+                    quant_w("o")
                 gate_t("g", m)
                 gate_o(2 * m)
                 gate_o(2 * m + 1)

@@ -19,6 +19,7 @@ P = 128
 NQ = T // 2
 V_TAIL = 1
 V_BLOCKS = 1
+ZB = 3
 LEAD = 3
 XCH = (2, 6, 8, 8, 8)
 PRODS = ((0, 1), (1, 1), (2, 2), (4, 4), (8, 4), (12, 4), (16, 4), (20, 4), (24, 4), (28, 4))
@@ -35,6 +36,7 @@ def tile_lstmlayer_kernel(tc, input_bytes, input_scale, h0, c0, noise, W_ih, W_h
         ps_tp = ctx.enter_context(tc.psum_pool(name="ps_tp", bufs=1))
         ps_mm = ctx.enter_context(tc.psum_pool(name="ps_mm", bufs=3))
         ps_cn = ctx.enter_context(tc.psum_pool(name="ps_cn", bufs=1))
+        ztp = ctx.enter_context(tc.tile_pool(name="ztp", bufs=1))
 
         sc4 = const.tile([P, 4, I], F32, name="sc4")
         xb = []
@@ -58,6 +60,9 @@ def tile_lstmlayer_kernel(tc, input_bytes, input_scale, h0, c0, noise, W_ih, W_h
         ident_f = const.tile([P, P], F32, name="ident_f")
 
         wgs = {}
+        fis = []
+        cgs = []
+        c0T_ps = ps_cn.tile([P, 4, P], F32, name="c0T_ps")
 
         def quant_w(x):
             cols = slice(ROWS[x] * 512, (ROWS[x] + 1) * 512)
@@ -104,13 +109,20 @@ def tile_lstmlayer_kernel(tc, input_bytes, input_scale, h0, c0, noise, W_ih, W_h
             load_x(4)
             load_w(whh, whh_v, "o")
             load_w(wih, wih_v, "o")
+            nc.scalar.dma_start(out=c0_sb[:], in_=c0)
             nc.scalar.dma_start(out=bt[0:1, :], in_=b_ih.rearrange("(o n) -> o n", o=1))
             nc.scalar.dma_start(out=bt[1:2, :], in_=b_hh.rearrange("(o n) -> o n", o=1))
-            nc.scalar.dma_start(out=c0_sb[:], in_=c0)
             nc.scalar.dma_start(out=nz_sb[:], in_=noise)
 
             make_identity(nc, ident_b[:])
             make_identity(nc, ident_f[:])
+
+            for jt in range(4):
+                nc.tensor.matmul(c0T_ps[:, jt, :], lhsT=c0_sb[:, jt * P:(jt + 1) * P], rhs=ident_b[:], start=True, stop=True)
+            for k in range(ZB):
+                fis.append(ztp.tile([P, 2, 4, 2, P], F32, name="fi%d" % k))
+                cgs.append(ztp.tile([P, 2, 4, 2, P], F32, name="cg%d" % k))
+                nc.scalar.copy(out=cgs[k][:, 0, V_BLOCKS:4, :, :], in_=c0T_ps[:, V_BLOCKS:4, :].unsqueeze(2).to_broadcast([P, 4 - V_BLOCKS, 2, P]))
 
             nc.scalar.copy(out=sc4[:, 1, :], in_=sc4[:, 0, :])
             nc.scalar.copy(out=sc4[:, 2:4, :], in_=sc4[:, 0:2, :])
@@ -169,16 +181,9 @@ def tile_lstmlayer_kernel(tc, input_bytes, input_scale, h0, c0, noise, W_ih, W_h
                     quant_w(x)
 
         ps_c = ctx.enter_context(tc.psum_pool(name="ps_c", bufs=2))
-        ztp = ctx.enter_context(tc.tile_pool(name="ztp", bufs=3))
         zop = ctx.enter_context(tc.tile_pool(name="zop", bufs=6))
         tcp = ctx.enter_context(tc.tile_pool(name="tcp", bufs=2))
 
-        c0T_ps = ps_cn.tile([P, 4, P], F32, name="c0T_ps")
-        for jt in range(4):
-            nc.tensor.matmul(c0T_ps[:, jt, :], lhsT=c0_sb[:, jt * P:(jt + 1) * P], rhs=ident_b[:], start=True, stop=True)
-        c0T2 = const.tile([P, 4, 2, P], F32, name="c0T2")
-        for j in range(2):
-            nc.scalar.copy(out=c0T2[:, :, j, :], in_=c0T_ps[:])
         nz_ps = ps_cn.tile([P, H], F32, name="nz_ps")
         nc.tensor.matmul(nz_ps[:], lhsT=ident_b[:], rhs=nz_sb[:], start=True, stop=True)
 
@@ -227,10 +232,7 @@ def tile_lstmlayer_kernel(tc, input_bytes, input_scale, h0, c0, noise, W_ih, W_h
         def gate_t(x, m):
             if not ok(m):
                 return
-            if m not in zts:
-                zt_new = ztp.tile([P, 3, 4, 2, P], F32, tag="zt")
-                zts[m] = zt_new
-            zt = zts[m]
+            zt = cgs[m % ZB][:, 1] if x == "g" else fis[m % ZB][:, SLOT[x]]
             gs = SLOT[x]
             qc = slice(m * 256, (m + 1) * 256)
             for half in range(2):
@@ -244,13 +246,13 @@ def tile_lstmlayer_kernel(tc, input_bytes, input_scale, h0, c0, noise, W_ih, W_h
                         start=True, stop=True,
                     )
                 nc.vector.tensor_tensor(
-                    out=zt[:, gs, 2 * half:2 * half + 2, :, :], in0=acc[:],
+                    out=zt[:, 2 * half:2 * half + 2, :, :], in0=acc[:],
                     in1=ghbT[:, gs, 2 * half:2 * half + 2, :].unsqueeze(2).to_broadcast([P, 2, 2, P]), op=ALU.add,
                 )
             if x == "g":
-                nc.scalar.activation(out=zt[:, gs, :, :, :], in_=zt[:, gs, :, :, :], func=ACT.Tanh)
+                nc.scalar.activation(out=zt, in_=zt, func=ACT.Tanh)
             if x == "i":
-                fi = zt[:, 0:2, :, :, :].rearrange("p s j t b -> p (s j t b)")
+                fi = fis[m % ZB][:].rearrange("p s j t b -> p (s j t b)")
                 nc.scalar.activation(out=fi, in_=fi, func=ACT.Sigmoid)
 
         def gate_o(t):
@@ -276,16 +278,16 @@ def tile_lstmlayer_kernel(tc, input_bytes, input_scale, h0, c0, noise, W_ih, W_h
 
         def op_v(m):
             if ok(m):
-                f_t = zts[m][:, SLOT["f"], :, :, :]
+                f_t = fis[m % ZB][:, 0]
                 vj = 4 if m >= NQ - V_TAIL else V_BLOCKS
                 nc.vector.tensor_tensor(out=f_t[:, 0:vj], in0=f_t[:, 0:vj], in1=c0T_ps[:, 0:vj, :].unsqueeze(2).to_broadcast([P, vj, 2, P]), op=ALU.mult)
-                if vj < 4:
-                    nc.gpsimd.tensor_tensor(out=f_t[:, vj:4], in0=f_t[:, vj:4], in1=c0T2[:, vj:4], op=ALU.mult)
 
         def op_u(m):
             if ok(m):
-                i_t = zts[m][:, SLOT["i"], :, :, :]
-                eng(m).tensor_tensor(out=i_t, in0=i_t, in1=zts[m][:, SLOT["g"], :, :, :], op=ALU.mult)
+                vj = 4 if m >= NQ - V_TAIL else V_BLOCKS
+                a = fis[m % ZB][:].rearrange("p s j t b -> p (s j) t b")
+                b = cgs[m % ZB][:].rearrange("p s j t b -> p (s j) t b")
+                eng(m).tensor_tensor(out=a[:, vj:8], in0=a[:, vj:8], in1=b[:, vj:8], op=ALU.mult)
 
         def op_c(m):
             if not ok(m):
@@ -295,7 +297,7 @@ def tile_lstmlayer_kernel(tc, input_bytes, input_scale, h0, c0, noise, W_ih, W_h
                 cps[2 * m + j] = cp
                 for jt in range(4):
                     for x in "fi":
-                        nc.tensor.matmul(cp[:, jt * P:(jt + 1) * P], lhsT=zts[m][:, SLOT[x], jt, j, :], rhs=ident_f[:], is_transpose=True, start=(x == "f"), stop=(x == "i"))
+                        nc.tensor.matmul(cp[:, jt * P:(jt + 1) * P], lhsT=fis[m % ZB][:, SLOT[x], jt, j, :], rhs=ident_f[:], is_transpose=True, start=(x == "f"), stop=(x == "i"))
 
         def op_th(m):
             if not ok(m):

@@ -39,6 +39,7 @@ def tile_lstmlayer_kernel(tc, input_bytes, input_scale, h0, c0, noise, W_ih, W_h
         ztp = ctx.enter_context(tc.tile_pool(name="ztp", bufs=1))
 
         sc4 = const.tile([P, 4, I], F32, name="sc4")
+        sc_col = const.tile([P, 4], F32, name="sc_col")
         xb = []
         xat = []
         for c in range(len(XCH)):
@@ -83,7 +84,7 @@ def tile_lstmlayer_kernel(tc, input_bytes, input_scale, h0, c0, noise, W_ih, W_h
             h0T = whead.tile([P, 4, P], BF16, name="h0T")
             whhT = whead.tile([P, 4, 4 * H], BF16, name="whhT")
 
-            nc.scalar.dma_start(out=sc4[:, 0, :], in_=input_scale.rearrange("a b k -> (a b k)").partition_broadcast(P))
+            nc.scalar.dma_start(out=sc_col[:], in_=input_scale.rearrange("a b (p t) -> p (a b t)", t=4))
             nc.vector.memset(warm[:], 0.0)
             nc.vector.memset(bt[:], 0.0)
             nc.vector.memset(ones[:], 1.0)
@@ -114,8 +115,15 @@ def tile_lstmlayer_kernel(tc, input_bytes, input_scale, h0, c0, noise, W_ih, W_h
             nc.scalar.dma_start(out=bt[1:2, :], in_=b_hh.rearrange("(o n) -> o n", o=1))
             nc.scalar.dma_start(out=nz_sb[:], in_=noise)
 
-            make_identity(nc, ident_b[:])
             make_identity(nc, ident_f[:])
+            make_identity(nc, ident_b[:])
+
+            pt_s = ps_hd.tile([P, 4, P], F32, tag="hd")
+            for t in range(4):
+                nc.tensor.transpose(pt_s[:, t, :], sc_col[:, t:t + 1].to_broadcast([P, P]), ident_f[:])
+            nc.scalar.copy(out=sc4[:, 0, :].rearrange("c (p t) -> c p t", t=4), in_=pt_s[:].rearrange("c t p -> c p t"))
+            nc.scalar.copy(out=sc4[:, 1, :], in_=sc4[:, 0, :])
+            nc.scalar.copy(out=sc4[:, 2:4, :], in_=sc4[:, 0:2, :])
 
             for jt in range(4):
                 nc.tensor.matmul(c0T_ps[:, jt, :], lhsT=c0_sb[:, jt * P:(jt + 1) * P], rhs=ident_b[:], start=True, stop=True)
@@ -124,8 +132,6 @@ def tile_lstmlayer_kernel(tc, input_bytes, input_scale, h0, c0, noise, W_ih, W_h
                 cgs.append(ztp.tile([P, 2, 4, 2, P], F32, name="cg%d" % k))
                 nc.scalar.copy(out=cgs[k][:, 0, V_BLOCKS:4, :, :], in_=c0T_ps[:, V_BLOCKS:4, :].unsqueeze(2).to_broadcast([P, 4 - V_BLOCKS, 2, P]))
 
-            nc.scalar.copy(out=sc4[:, 1, :], in_=sc4[:, 0, :])
-            nc.scalar.copy(out=sc4[:, 2:4, :], in_=sc4[:, 0:2, :])
 
             for t0, n in PRODS:
                 c, j = xat[t0]

@@ -34,7 +34,7 @@ def tile_lstmlayer_kernel(tc, input_bytes, input_scale, h0, c0, noise, W_ih, W_h
         xbytes = ctx.enter_context(tc.tile_pool(name="xbytes", bufs=1))
         stage = ctx.enter_context(tc.tile_pool(name="stage", bufs=2))
         ps_tp = ctx.enter_context(tc.psum_pool(name="ps_tp", bufs=1))
-        ps_mm = ctx.enter_context(tc.psum_pool(name="ps_mm", bufs=3))
+        ps_mm = ctx.enter_context(tc.psum_pool(name="ps_mm", bufs=4))
         ps_cn = ctx.enter_context(tc.psum_pool(name="ps_cn", bufs=1))
         ztp = ctx.enter_context(tc.tile_pool(name="ztp", bufs=1))
 
@@ -63,7 +63,9 @@ def tile_lstmlayer_kernel(tc, input_bytes, input_scale, h0, c0, noise, W_ih, W_h
         wgs = {}
         fis = []
         cgs = []
-        c0T_ps = ps_cn.tile([P, 4, P], F32, name="c0T_ps")
+        cn_ps = ps_cn.tile([P, 8, P], BF16, name="cn_ps")
+        c0T_ps = cn_ps[:, 4:8, :]
+        nz_ps = cn_ps[:, 0:4, :].rearrange("p a b -> p (a b)")
 
         def quant_w(x):
             cols = slice(ROWS[x] * 512, (ROWS[x] + 1) * 512)
@@ -190,8 +192,7 @@ def tile_lstmlayer_kernel(tc, input_bytes, input_scale, h0, c0, noise, W_ih, W_h
         zop = ctx.enter_context(tc.tile_pool(name="zop", bufs=6))
         tcp = ctx.enter_context(tc.tile_pool(name="tcp", bufs=2))
 
-        nz_ps = ps_cn.tile([P, H], F32, name="nz_ps")
-        nc.tensor.matmul(nz_ps[:], lhsT=ident_b[:], rhs=nz_sb[:], start=True, stop=True)
+        nc.tensor.matmul(nz_ps, lhsT=ident_b[:], rhs=nz_sb[:], start=True, stop=True)
 
         pts = {}
         xgs = {}
@@ -235,13 +236,13 @@ def tile_lstmlayer_kernel(tc, input_bytes, input_scale, h0, c0, noise, W_ih, W_h
                 return nc.gpsimd
             return nc.vector
 
-        def gate_t(x, m):
+        def gate_t(x, m, halves=(0, 1)):
             if not ok(m):
                 return
             zt = cgs[m % ZB][:, 1] if x == "g" else fis[m % ZB][:, SLOT[x]]
             gs = SLOT[x]
             qc = slice(m * 256, (m + 1) * 256)
-            for half in range(2):
+            for half in halves:
                 acc = ps_mm.tile([P, 2, 2, P], F32, tag="mm")
                 for e in range(2):
                     jc = slice(ROWS[x] * 512 + (2 * half + e) * P, ROWS[x] * 512 + (2 * half + e + 1) * P)
@@ -257,7 +258,7 @@ def tile_lstmlayer_kernel(tc, input_bytes, input_scale, h0, c0, noise, W_ih, W_h
                 )
             if x == "g":
                 nc.scalar.activation(out=zt, in_=zt, func=ACT.Tanh)
-            if x == "i":
+            if x == "i" and 1 in halves:
                 fi = fis[m % ZB][:].rearrange("p s j t b -> p (s j t b)")
                 nc.scalar.activation(out=fi, in_=fi, func=ACT.Sigmoid)
 
@@ -325,7 +326,7 @@ def tile_lstmlayer_kernel(tc, input_bytes, input_scale, h0, c0, noise, W_ih, W_h
             if not ok(m):
                 return
             zo = zos[m]
-            nc.vector.tensor_tensor(out=zo[:], in0=zo[:], in1=nz_ps[:].unsqueeze(1).to_broadcast([P, 2, H]), op=ALU.add)
+            nc.vector.tensor_tensor(out=zo[:], in0=zo[:], in1=nz_ps.unsqueeze(1).to_broadcast([P, 2, H]), op=ALU.add)
             nc.sync.dma_start(out=out_0[2 * m:2 * m + 2].rearrange("t b j -> b t j"), in_=zo[:])
             if m == NQ - 1:
                 nc.sync.dma_start(out=out_1[0], in_=zo[:, 1, :])
@@ -342,12 +343,13 @@ def tile_lstmlayer_kernel(tc, input_bytes, input_scale, h0, c0, noise, W_ih, W_h
                 op_v(m - 1)
                 op_u(m - 1)
                 gate_t("f", m)
+                gate_t("i", m, (0,))
                 op_c(m - 2)
                 turn_t(m + LEAD)
                 turn_e(m + LEAD)
                 op_th(m - 2)
                 op_w(m - 2)
-                gate_t("i", m)
+                gate_t("i", m, (1,))
                 if m == 0:
                     quant_w("o")
                 gate_t("g", m)

from contextlib import ExitStack

import concourse.mybir as mybir
from concourse.masks import make_identity

T, B, I, H = 32, 128, 512, 512
FLOPS = 2 * T * B * 4 * H * I + 2 * B * 4 * H * H

F32 = mybir.dt.float32
BF16 = mybir.dt.bfloat16
U32 = mybir.dt.uint32
U8 = mybir.dt.uint8
FP8 = mybir.dt.float8_e4m3fn
FP8X4 = mybir.dt.float8_e4m3fn_x4
ALU = mybir.AluOpType
ACT = mybir.ActivationFunctionType

P = 128
NQ = T // 2
V_TAIL = 1
V_BLOCKS = 1
ZB = 3
LEAD = 3
XCH = (2, 6, 8, 8, 8)
PRODS = ((0, 1), (1, 1), (2, 2), (4, 4), (8, 4), (12, 4), (16, 4), (20, 4), (24, 4), (28, 4))
ROWS = {"i": 0, "f": 1, "g": 2, "o": 3}
SLOT = {"f": 0, "i": 1, "g": 2}


def tile_lstmlayer_kernel(tc, input_bytes, input_scale, h0, c0, noise, W_ih, W_hh, b_ih, b_hh, out_0, out_1):
    nc = tc.nc
    with ExitStack() as ctx:
        const = ctx.enter_context(tc.tile_pool(name="const", bufs=1))
        xbytes = ctx.enter_context(tc.tile_pool(name="xbytes", bufs=1))
        stage = ctx.enter_context(tc.tile_pool(name="stage", bufs=2))
        ps_tp = ctx.enter_context(tc.psum_pool(name="ps_tp", bufs=1))
        ps_mm = ctx.enter_context(tc.psum_pool(name="ps_mm", bufs=4))
        ps_cn = ctx.enter_context(tc.psum_pool(name="ps_cn", bufs=1))
        ztp = ctx.enter_context(tc.tile_pool(name="ztp", bufs=1))

        sc4 = const.tile([P, 4, I], F32, name="sc4")
        sc_col = const.tile([P, 4], F32, name="sc_col")
        xb = []
        xat = []
        for c in range(len(XCH)):
            xb.append(xbytes.tile([P, XCH[c], I], U8, name="xb%d" % c))
            for j in range(XCH[c]):
                xat.append((c, j))
        c0_sb = const.tile([P, H], BF16, name="c0_sb")
        nz_sb = const.tile([P, H], BF16, name="nz_sb")
        ones = const.tile([P, P], BF16, name="ones")
        warm = const.tile([P, 2], F32, name="warm")
        ghbT = const.tile([P, 3, 4, P], F32, name="ghbT")
        ghbo = const.tile([P, H], F32, name="ghbo")
        wcodes = const.tile([P, 4 * H], U32, name="wcodes", align_bytes=64)
        wsc = const.tile([P, 4 * H], U8, name="wsc", align_bytes=64)
        xcodes = const.tile([P, T * B], U32, name="xcodes", align_bytes=64)
        xsc = const.tile([P, T * B], U8, name="xsc", align_bytes=64)
        xs = const.tile([P, T, I], BF16, name="xs")
        ident_b = const.tile([P, P], BF16, name="ident_b")
        ident_f = const.tile([P, P], F32, name="ident_f")

        wgs = {}
        fis = []
        cgs = []
        cn_ps = ps_cn.tile([P, 8, P], BF16, name="cn_ps")
        c0T_ps = cn_ps[:, 4:8, :]
        nz_ps = cn_ps[:, 0:4, :].rearrange("p a b -> p (a b)")

        def quant_w(x):
            cols = slice(ROWS[x] * 512, (ROWS[x] + 1) * 512)
            nc.vector.quantize_mx(out=wcodes[:, cols].bitcast(FP8X4), scales=wsc[:, cols], in_=wgs[x][:])

        def load_x(c):
            t0 = sum(XCH[:c])
            nc.sync.dma_start(out=xb[c][:], in_=input_bytes[t0:t0 + XCH[c]].rearrange("t b k -> b t k"))

        with tc.tile_pool(name="whead", bufs=1) as whead, tc.psum_pool(name="ps_hd", bufs=2) as ps_hd:
            whh = {}
            wih = {}
            for x in "figo":
                whh[x] = whead.tile([P, 4, H], BF16, name="whh_" + x)
                wih[x] = whead.tile([P, 4, I], BF16, name="wih_" + x)
            h0_sb = whead.tile([P, H], BF16, name="h0_sb")
            bt = whead.tile([P, 4 * H], BF16, name="bt")
            h0T = whead.tile([P, 4, P], BF16, name="h0T")
            whhT = whead.tile([P, 4, 4 * H], BF16, name="whhT")

            nc.scalar.dma_start(out=sc_col[:], in_=input_scale.rearrange("a b (p t) -> p (a b t)", t=4))
            nc.vector.memset(warm[:], 0.0)
            nc.vector.memset(bt[:], 0.0)
            nc.vector.memset(ones[:], 1.0)
            nc.scalar.activation(out=warm[:, 1:2], in_=warm[:, 0:1], func=ACT.Sigmoid)

            whh_v = W_hh.rearrange("(r p) k -> p r k", p=P)
            wih_v = W_ih.rearrange("(r p) k -> p r k", p=P)

            def load_w(dst, view, x):
                nc.sync.dma_start(out=dst[x][:], in_=view[:, 4 * ROWS[x]:4 * ROWS[x] + 4, :])

            load_x(0)
            load_x(1)
            nc.sync.dma_start(out=h0_sb[:], in_=h0)
            load_w(whh, whh_v, "f")
            load_w(wih, wih_v, "f")
            load_x(2)
            load_w(whh, whh_v, "i")
            load_w(wih, wih_v, "i")
            load_x(3)
            load_w(whh, whh_v, "g")
            load_w(wih, wih_v, "g")
            load_x(4)
            load_w(whh, whh_v, "o")
            load_w(wih, wih_v, "o")
            nc.scalar.dma_start(out=c0_sb[:], in_=c0)
            nc.scalar.dma_start(out=bt[0:1, :], in_=b_ih.rearrange("(o n) -> o n", o=1))
            nc.scalar.dma_start(out=bt[1:2, :], in_=b_hh.rearrange("(o n) -> o n", o=1))
            nc.scalar.dma_start(out=nz_sb[:], in_=noise)

            make_identity(nc, ident_f[:])
            make_identity(nc, ident_b[:])

            pt_s = ps_hd.tile([P, 4, P], F32, tag="hd")
            for t in range(4):
                nc.tensor.transpose(pt_s[:, t, :], sc_col[:, t:t + 1].to_broadcast([P, P]), ident_f[:])
            nc.scalar.copy(out=sc4[:, 0, :].rearrange("c (p t) -> c p t", t=4), in_=pt_s[:].rearrange("c t p -> c p t"))
            nc.scalar.copy(out=sc4[:, 1, :], in_=sc4[:, 0, :])
            nc.scalar.copy(out=sc4[:, 2:4, :], in_=sc4[:, 0:2, :])

            for jt in range(4):
                nc.tensor.matmul(c0T_ps[:, jt, :], lhsT=c0_sb[:, jt * P:(jt + 1) * P], rhs=ident_b[:], start=True, stop=True)
            for k in range(ZB):
                fis.append(ztp.tile([P, 2, 4, 2, P], F32, name="fi%d" % k))
                cgs.append(ztp.tile([P, 2, 4, 2, P], F32, name="cg%d" % k))
                nc.scalar.copy(out=cgs[k][:, 0, V_BLOCKS:4, :, :], in_=c0T_ps[:, V_BLOCKS:4, :].unsqueeze(2).to_broadcast([P, 4 - V_BLOCKS, 2, P]))


            for t0, n in PRODS:
                c, j = xat[t0]
                nc.vector.tensor_tensor(
                    out=xs[:, t0:t0 + n, :].rearrange("p n k -> p (n k)"),
                    in0=xb[c][:, j:j + n, :].rearrange("p n k -> p (n k)").bitcast(FP8),
                    in1=sc4[:, 0:n, :].rearrange("p n k -> p (n k)"),
                    op=ALU.mult,
                )

            pt_h = ps_hd.tile([P, 4, P], BF16, tag="hd")
            for kt in range(4):
                nc.tensor.transpose(pt_h[:, kt, :], h0_sb[:, kt * P:(kt + 1) * P], ident_b[:])
            nc.scalar.copy(out=h0T[:], in_=pt_h[:])

            for x in "figo":
                cols = slice(ROWS[x] * 512, (ROWS[x] + 1) * 512)
                for half in range(2):
                    pt_w = ps_hd.tile([P, 2, 512], BF16, tag="hd")
                    for kk in range(2):
                        kt = 2 * half + kk
                        for r in range(4):
                            nc.tensor.transpose(pt_w[:, kk, r * P:(r + 1) * P], whh[x][:, r, kt * P:(kt + 1) * P], ident_b[:])
                    nc.scalar.copy(out=whhT[:, 2 * half:2 * half + 2, cols], in_=pt_w[:])
                if x == "o":
                    gp = ps_mm.tile([P, 512], F32, tag="mm")
                    for kt in range(4):
                        nc.tensor.matmul(gp[:], lhsT=h0T[:, kt, :], rhs=whhT[:, kt, cols], start=(kt == 0), stop=False)
                    nc.tensor.matmul(gp[:], lhsT=ones[:], rhs=bt[:, cols], start=False, stop=True)
                    nc.scalar.copy(out=ghbo[:], in_=gp[:])
                else:
                    gq = ps_mm.tile([P, 4, P], F32, tag="mm")
                    for jt in range(4):
                        jc = slice(cols.start + jt * P, cols.start + (jt + 1) * P)
                        for kt in range(4):
                            nc.tensor.matmul(gq[:, jt, :], lhsT=whhT[:, kt, jc], rhs=h0T[:, kt, :], start=(kt == 0), stop=False)
                        nc.tensor.matmul(gq[:, jt, :], lhsT=bt[:, jc], rhs=ones[:], start=False, stop=True)
                    nc.scalar.copy(out=ghbT[:, SLOT[x], :, :], in_=gq[:])
                wg = stage.tile([P, 2048], BF16, tag="wg", align_bytes=64)
                wwords = wih[x][:].bitcast(F32)
                wgw = wg[:].bitcast(F32)
                for rp in range(2):
                    pt_i = ps_hd.tile([P, 2, 2, P], F32, tag="hd")
                    for r2 in range(2):
                        for u in range(2):
                            nc.tensor.transpose(pt_i[:, r2, u, :], wwords[:, 2 * rp + r2, u:256:2], ident_f[:])
                    nc.scalar.copy(
                        out=wgw[:, rp * 512:(rp + 1) * 512].rearrange("p (r n u) -> p r n u", r=2, u=2),
                        in_=pt_i[:].rearrange("p r u n -> p r n u"),
                    )
                wgs[x] = wg
                if x != "o":
                    quant_w(x)

        ps_c = ctx.enter_context(tc.psum_pool(name="ps_c", bufs=2))
        zop = ctx.enter_context(tc.tile_pool(name="zop", bufs=6))
        tcp = ctx.enter_context(tc.tile_pool(name="tcp", bufs=2))

        nc.tensor.matmul(nz_ps, lhsT=ident_b[:], rhs=nz_sb[:], start=True, stop=True)

        pts = {}
        xgs = {}

        def ok(m):
            return 0 <= m < NQ

        def turn_t(q):
            if not ok(q):
                return
            xwords = xs[:, 2 * q:2 * q + 2, :].bitcast(F32)
            pt_x = ps_tp.tile([P, 2, 2, P], F32, tag="tp")
            pts[q] = pt_x
            for j in range(2):
                for u in range(2):
                    nc.tensor.transpose(pt_x[:, j, u, :], xwords[:, j, u:256:2], ident_f[:])

        def turn_e(q):
            if not ok(q):
                return
            xg = stage.tile([P, 1024], BF16, tag="xg", align_bytes=64)
            xgs[q] = xg
            nc.scalar.copy(
                out=xg[:].bitcast(F32).rearrange("p (r n u) -> p r n u", r=2, u=2),
                in_=pts[q][:].rearrange("p r u n -> p r n u"),
            )

        def turn_q(q):
            if not ok(q):
                return
            qc = slice(q * 256, (q + 1) * 256)
            nc.vector.quantize_mx(out=xcodes[:, qc].bitcast(FP8X4), scales=xsc[:, qc], in_=xgs[q][:])

        zts = {}
        zos = {}
        tcs = {}
        cps = {}

        def eng(m):
            if m < NQ - V_TAIL:
                return nc.gpsimd
            return nc.vector

        def gate_t(x, m, halves=(0, 1)):
            if not ok(m):
                return
            zt = cgs[m % ZB][:, 1] if x == "g" else fis[m % ZB][:, SLOT[x]]
            gs = SLOT[x]
            qc = slice(m * 256, (m + 1) * 256)
            for half in halves:
                acc = ps_mm.tile([P, 2, 2, P], F32, tag="mm")
                for e in range(2):
                    jc = slice(ROWS[x] * 512 + (2 * half + e) * P, ROWS[x] * 512 + (2 * half + e + 1) * P)
                    nc.tensor.matmul_mx(
                        out=acc[:, e, :, :].rearrange("p t b -> p (t b)"),
                        lhsT=wcodes[:, jc].bitcast(FP8X4), lhsT_scale=wsc[:, jc],
                        rhs=xcodes[:, qc].bitcast(FP8X4), rhs_scale=xsc[:, qc],
                        start=True, stop=True,
                    )
                nc.vector.tensor_tensor(
                    out=zt[:, 2 * half:2 * half + 2, :, :], in0=acc[:],
                    in1=ghbT[:, gs, 2 * half:2 * half + 2, :].unsqueeze(2).to_broadcast([P, 2, 2, P]), op=ALU.add,
                )
            if x == "g":
                nc.scalar.activation(out=zt, in_=zt, func=ACT.Tanh)
            if x == "i" and 1 in halves:
                fi = fis[m % ZB][:].rearrange("p s j t b -> p (s j t b)")
                nc.scalar.activation(out=fi, in_=fi, func=ACT.Sigmoid)

        def gate_o(t):
            m = t // 2
            if not ok(m):
                return
            if m not in zos:
                zo_new = zop.tile([P, 2, H], F32, tag="zo")
                zos[m] = zo_new
            zo = zos[m]
            tcols = slice(t * P, (t + 1) * P)
            cols = slice(ROWS["o"] * 512, (ROWS["o"] + 1) * 512)
            acc = ps_mm.tile([P, 512], F32, tag="mm")
            nc.tensor.matmul_mx(
                out=acc[:],
                lhsT=xcodes[:, tcols].bitcast(FP8X4), lhsT_scale=xsc[:, tcols],
                rhs=wcodes[:, cols].bitcast(FP8X4), rhs_scale=wsc[:, cols],
                start=True, stop=True,
            )
            nc.vector.tensor_tensor(out=zo[:, t % 2, :], in0=acc[:], in1=ghbo[:], op=ALU.add)
            if t % 2 == 1:
                nc.scalar.activation(out=zo[:], in_=zo[:], func=ACT.Sigmoid)

        def op_v(m):
            if ok(m):
                f_t = fis[m % ZB][:, 0]
                vj = 4 if m >= NQ - V_TAIL else V_BLOCKS
                nc.vector.tensor_tensor(out=f_t[:, 0:vj], in0=f_t[:, 0:vj], in1=c0T_ps[:, 0:vj, :].unsqueeze(2).to_broadcast([P, vj, 2, P]), op=ALU.mult)

        def op_u(m):
            if ok(m):
                vj = 4 if m >= NQ - V_TAIL else V_BLOCKS
                a = fis[m % ZB][:].rearrange("p s j t b -> p (s j) t b")
                b = cgs[m % ZB][:].rearrange("p s j t b -> p (s j) t b")
                eng(m).tensor_tensor(out=a[:, vj:8], in0=a[:, vj:8], in1=b[:, vj:8], op=ALU.mult)

        def op_c(m):
            if not ok(m):
                return
            for j in range(2):
                cp = ps_c.tile([P, H], F32, tag="c")
                cps[2 * m + j] = cp
                for jt in range(4):
                    for x in "fi":
                        nc.tensor.matmul(cp[:, jt * P:(jt + 1) * P], lhsT=fis[m % ZB][:, SLOT[x], jt, j, :], rhs=ident_f[:], is_transpose=True, start=(x == "f"), stop=(x == "i"))

        def op_th(m):
            if not ok(m):
                return
            tc_new = tcp.tile([P, 2, H], F32, tag="tc")
            tcs[m] = tc_new
            for j in range(2):
                nc.scalar.activation(out=tc_new[:, j, :], in_=cps[2 * m + j][:], func=ACT.Tanh)
            if m == NQ - 1:
                c_last = const.tile([P, H], F32, name="c_last")
                nc.scalar.copy(out=c_last[:], in_=cps[2 * m + 1][:])
                nc.sync.dma_start(out=out_1[1], in_=c_last[:])

        def op_w(m):
            if ok(m):
                eng(m).tensor_tensor(out=zos[m][:], in0=zos[m][:], in1=tcs[m][:], op=ALU.mult)

        def op_h(m):
            if not ok(m):
                return
            zo = zos[m]
            nc.vector.tensor_tensor(out=zo[:], in0=zo[:], in1=nz_ps.unsqueeze(1).to_broadcast([P, 2, H]), op=ALU.add)
            nc.sync.dma_start(out=out_0[2 * m:2 * m + 2].rearrange("t b j -> b t j"), in_=zo[:])
            if m == NQ - 1:
                nc.sync.dma_start(out=out_1[0], in_=zo[:, 1, :])

        for q in range(LEAD):
            turn_t(q)
            turn_e(q)
            if q < LEAD - 1:
                turn_q(q)
        with tc.manual_schedule():
            for m in range(NQ + 5):
                op_h(m - 4)
                turn_q(m + LEAD - 1)
                op_v(m - 1)
                op_u(m - 1)
                gate_t("f", m)
                gate_t("i", m, (0,))
                op_c(m - 2)
                turn_t(m + LEAD)
                turn_e(m + LEAD)
                op_th(m - 2)
                op_w(m - 2)
                gate_t("i", m, (1,))
                if m == 0:
                    quant_w("o")
                gate_t("g", m)
                gate_o(2 * m)
                gate_o(2 * m + 1)
